import numpy as np
import ml_dtypes


def mxq(x, axis, fmt="e4m3"):
    dtype, down = {"e4m3": (ml_dtypes.float8_e4m3fn, 7), "e5m2": (ml_dtypes.float8_e5m2, 14)}[fmt]
    v = np.moveaxis(np.asarray(x, np.float32).astype(ml_dtypes.bfloat16).astype(np.float64), axis, -1)
    blocks = v.reshape(v.shape[:-1] + (-1, 32))
    amax = np.abs(blocks).max(-1, keepdims=True)
    byte = np.maximum(np.where(amax > 0, np.frexp(amax)[1] - 1 + 127, 0) - down, 1)
    scale = np.exp2(byte - 127.0)
    codes = (blocks / scale).astype(np.float32).astype(dtype).astype(np.float64)
    return np.moveaxis((codes * scale).reshape(v.shape), -1, axis)


WIDE = False


def mx_kscale(k):
    if not WIDE:
        return np.ones(k)
    levels = np.array([10, -10, 5, -5, 0])
    a = np.random.permutation(np.resize(levels, k // 512 * 4)).reshape(k // 512, 4)
    idx = np.arange(k)
    return np.exp2(a[idx // 512, idx % 128 // 32])


BF16 = ml_dtypes.bfloat16


def bf(x):
    return np.asarray(x, np.float32).astype(BF16)


def f64(x):
    return np.asarray(x).astype(np.float64)


E2M1 = np.array([0.0, 0.5, 1.0, 1.5, 2.0, 3.0, 4.0, 6.0, -0.0, -0.5, -1.0, -1.5, -2.0, -3.0, -4.0, -6.0])


def pack_weight(w, fmt):
    k, n = w.shape
    w = f64(bf(w)).reshape(k // 32, 32, n)
    amax = np.abs(w).max(1)
    if fmt == "e4m3":
        byte = np.frexp(amax)[1] - 1 + 127 - 7
    else:
        mant, ex = np.frexp(amax / 6.0)
        byte = np.where(mant > 0.5, ex, ex - 1) + 127
    byte = np.clip(np.where(amax > 0, byte, 1), 1, 254)
    scaled = (w * np.exp2(127.0 - byte)[:, None, :]).reshape(k, n).astype(np.float32)
    by_word = np.ascontiguousarray(scaled.reshape(k // 512, 128, 4, n).transpose(0, 1, 3, 2))
    if fmt == "e4m3":
        words = by_word.astype(ml_dtypes.float8_e4m3fn).view(np.uint8)
    else:
        c = by_word.astype(ml_dtypes.float4_e2m1fn).view(np.uint8) & 0xF
        words = c[..., 0::2] | (c[..., 1::2] << 4)
    return np.ascontiguousarray(words), np.ascontiguousarray(byte.astype(np.uint8).reshape(k // 512, 16, n))


def unpack_weight(words, scales, fmt):
    g, p, n, _ = words.shape
    if fmt == "e4m3":
        vals = np.ascontiguousarray(words).view(ml_dtypes.float8_e4m3fn).astype(np.float64)
    else:
        nib = np.empty((g, p, n, 4), np.uint8)
        nib[..., 0::2] = words & 0xF
        nib[..., 1::2] = words >> 4
        vals = E2M1[nib]
    vals = vals * np.repeat(np.exp2(scales.astype(np.float64) - 127.0), 8, axis=1)[..., None]
    return vals.transpose(0, 1, 3, 2).reshape(g * 512, n)


B, CIN, COUT, H, W = 2, 16384, 1024, 8, 8


def setup_inputs():
    s = mx_kscale(CIN)
    x = np.random.standard_normal((B, CIN, H, W)) * s[None, :, None, None]
    weight = np.random.uniform(-1.0, 1.0, (CIN, COUT)) * np.sqrt(3.0 / CIN) / s[:, None]
    words, scales = pack_weight(weight, "e4m3")
    return {"x": bf(x), "weight_words": words, "weight_scales": scales}


def reference(x, weight_words, weight_scales):
    wq = unpack_weight(weight_words, weight_scales, "e4m3")
    xq = mxq(f64(x), 1, "e4m3")
    return np.einsum("io,bihw->bohw", wq, xq, optimize=True)

@@ -1,0 +1,106 @@
+from contextlib import ExitStack
+
+import concourse.mybir as mybir
+
+FP8X4 = mybir.dt.float8_e4m3fn_x4
+BF16 = mybir.dt.bfloat16
+F32 = mybir.dt.float32
+I32 = mybir.dt.int32
+U32 = mybir.dt.uint32
+U8 = mybir.dt.uint8
+
+P = 128
+PACK = 4
+K_PASS = P * PACK
+BATCH, CIN, COUT, PIXELS = 2, 16384, 1024, 64
+GROUPS = CIN // K_PASS
+COLS = BATCH * PIXELS
+O_TILES = COUT // P
+QUADRANTS = 4
+ROWS = 4
+STEP = 4
+STEPS = GROUPS // STEP
+
+FLOPS = 2 * CIN * COUT * COLS
+
+
+def tile_simpleconvolution_k_kernel(tc, x, weight_words, weight_scales, out):
+    nc = tc.nc
+    with ExitStack() as ctx:
+        keep = ctx.enter_context(tc.tile_pool(name="keep", bufs=1))
+        words_pool = ctx.enter_context(tc.tile_pool(name="words", bufs=STEPS))
+        raw_pool = ctx.enter_context(tc.tile_pool(name="raw", bufs=STEPS))
+        grouped_pool = ctx.enter_context(tc.tile_pool(name="grouped", bufs=2))
+        psum = ctx.enter_context(tc.psum_pool(name="psum", bufs=1))
+        ctx.enter_context(tc.manual_schedule())
+
+        w_scales = keep.tile([P, STEPS, COUT], U8, align_bytes=64)
+        nc.vector.memset(w_scales[:].bitcast(I32), 0)
+
+        x_raw_of = []
+        w_words_of = []
+        for step in range(STEPS):
+            g0 = step * STEP
+            x_raw = raw_pool.tile([P, STEP, BATCH, PACK * PIXELS], BF16)
+            for b in range(BATCH):
+                nc.sync.dma_start(
+                    out=x_raw[:, :, b, :],
+                    in_=x[b, g0 * K_PASS : (g0 + STEP) * K_PASS].rearrange(
+                        "(g p t) h w -> p g (t h w)", p=P, t=PACK
+                    ),
+                )
+            x_raw_of.append(x_raw)
+            for quad in range(QUADRANTS):
+                nc.sync.dma_start(
+                    out=w_scales[32 * quad : 32 * quad + STEP * ROWS, step, :].bitcast(I32),
+                    in_=weight_scales[g0 : g0 + STEP, ROWS * quad : ROWS * (quad + 1), :].bitcast(I32),
+                )
+            w_words = words_pool.tile([P, STEP, COUT], U32, align_bytes=64)
+            for j in range(STEP):
+                nc.sync.dma_start(
+                    out=w_words[:, j, :].bitcast(I32),
+                    in_=weight_words[g0 + j].rearrange("p n t -> p (n t)").bitcast(I32),
+                )
+            w_words_of.append(w_words)
+
+        x_codes = keep.tile([P, GROUPS, COLS], U32, align_bytes=64)
+        x_scales = keep.tile([P, GROUPS, COLS], U8, align_bytes=64)
+        for step in range(STEPS):
+            groups = slice(step * STEP, (step + 1) * STEP)
+            grouped = grouped_pool.tile([P, STEP * BATCH, PIXELS, PACK], BF16, align_bytes=64)
+            nc.vector.tensor_copy(
+                out=grouped[:],
+                in_=x_raw_of[step][:].rearrange("p g b (t s) -> p (g b) s t", t=PACK),
+            )
+            nc.vector.quantize_mx(
+                out=x_codes[:, groups, :].rearrange("p g c -> p (g c)").bitcast(FP8X4),
+                scales=x_scales[:, groups, :].rearrange("p g c -> p (g c)"),
+                in_=grouped[:].rearrange("p a s t -> p (a s t)"),
+            )
+
+        acc_of = [psum.tile([P, COLS], F32, name="acc%d" % o) for o in range(O_TILES)]
+        for g in range(GROUPS):
+            step, j = divmod(g, STEP)
+            for o in range(O_TILES):
+                o_cols = slice(o * P, (o + 1) * P)
+                nc.tensor.matmul_mx(
+                    out=acc_of[o][:],
+                    lhsT=w_words_of[step][:, j, o_cols].bitcast(FP8X4),
+                    lhsT_scale=w_scales[ROWS * j : P, step, o_cols],
+                    rhs=x_codes[:, g, :].bitcast(FP8X4),
+                    rhs_scale=x_scales[:, g, :],
+                    start=(g == 0),
+                    stop=(g == GROUPS - 1),
+                )
+
+        result = keep.tile([P, O_TILES, COLS], F32)
+        for o in range(O_TILES):
+            if o % 2 == 0:
+                nc.vector.tensor_copy(out=result[:, o, :], in_=acc_of[o][:])
+            else:
+                nc.scalar.copy(out=result[:, o, :], in_=acc_of[o][:])
+        for b in range(BATCH):
+            nc.sync.dma_start(
+                out=out[b].rearrange("(o p) h w -> p o (h w)", p=P),
+                in_=result[:, :, b * PIXELS : (b + 1) * PIXELS],
+            )

@@ -37,6 +37,14 @@ def tile_simpleconvolution_k_kernel(tc, x, weight_words, weight_scales, out):
         w_scales = keep.tile([P, STEPS, COUT], U8, align_bytes=64)
         nc.vector.memset(w_scales[:].bitcast(I32), 0)
 
+        for step in range(STEPS):
+            g0 = step * STEP
+            for quad in range(QUADRANTS):
+                nc.gpsimd.dma_start(
+                    out=w_scales[32 * quad : 32 * quad + STEP * ROWS, step, :].bitcast(F32),
+                    in_=weight_scales[g0 : g0 + STEP, ROWS * quad : ROWS * (quad + 1), :].bitcast(F32),
+                )
+
         x_raw_of = []
         w_words_of = []
         for step in range(STEPS):
@@ -50,11 +58,6 @@ def tile_simpleconvolution_k_kernel(tc, x, weight_words, weight_scales, out):
                     ),
                 )
             x_raw_of.append(x_raw)
-            for quad in range(QUADRANTS):
-                nc.sync.dma_start(
-                    out=w_scales[32 * quad : 32 * quad + STEP * ROWS, step, :].bitcast(I32),
-                    in_=weight_scales[g0 : g0 + STEP, ROWS * quad : ROWS * (quad + 1), :].bitcast(I32),
-                )
             w_words = words_pool.tile([P, STEP, COUT], U32, align_bytes=64)
             for j in range(STEP):
                 nc.sync.dma_start(

@@ -1,5 +1,4 @@
-from contextlib import ExitStack
-
+from concourse.masks import make_identity
 import concourse.mybir as mybir
 
 FP8X4 = mybir.dt.float8_e4m3fn_x4
@@ -21,89 +20,138 @@ ROWS = 4
 STEP = 4
 STEPS = GROUPS // STEP
 
+HALF = GROUPS // 2
+PIECES = P // HALF
+WORDS_C = P // PIECES
+PER_BANK = 4
+QUANT = 4
+
 FLOPS = 2 * CIN * COUT * COLS
 
 
 def tile_simpleconvolution_k_kernel(tc, x, weight_words, weight_scales, out):
     nc = tc.nc
-    with ExitStack() as ctx:
-        keep = ctx.enter_context(tc.tile_pool(name="keep", bufs=1))
-        words_pool = ctx.enter_context(tc.tile_pool(name="words", bufs=STEPS))
-        raw_pool = ctx.enter_context(tc.tile_pool(name="raw", bufs=STEPS))
-        grouped_pool = ctx.enter_context(tc.tile_pool(name="grouped", bufs=2))
-        psum = ctx.enter_context(tc.psum_pool(name="psum", bufs=1))
-        ctx.enter_context(tc.manual_schedule())
-
+    with tc.manual_schedule(), tc.tile_pool(name="keep", bufs=1) as keep:
         w_scales = keep.tile([P, STEPS, COUT], U8, align_bytes=64)
         nc.vector.memset(w_scales[:].bitcast(I32), 0)
-
+        identity = keep.tile([P, P], F32)
+        make_identity(nc, identity[:])
         for step in range(STEPS):
-            g0 = step * STEP
             for quad in range(QUADRANTS):
                 nc.gpsimd.dma_start(
                     out=w_scales[32 * quad : 32 * quad + STEP * ROWS, step, :].bitcast(F32),
-                    in_=weight_scales[g0 : g0 + STEP, ROWS * quad : ROWS * (quad + 1), :].bitcast(F32),
+                    in_=weight_scales[
+                        step * STEP : (step + 1) * STEP, ROWS * quad : ROWS * (quad + 1), :
+                    ].bitcast(F32),
                 )
 
-        x_raw_of = []
-        w_words_of = []
-        for step in range(STEPS):
-            g0 = step * STEP
-            x_raw = raw_pool.tile([P, STEP, BATCH, PACK * PIXELS], BF16)
-            for b in range(BATCH):
-                nc.sync.dma_start(
-                    out=x_raw[:, :, b, :],
-                    in_=x[b, g0 * K_PASS : (g0 + STEP) * K_PASS].rearrange(
-                        "(g p t) h w -> p g (t h w)", p=P, t=PACK
-                    ),
-                )
-            x_raw_of.append(x_raw)
-            w_words = words_pool.tile([P, STEP, COUT], U32, align_bytes=64)
-            for j in range(STEP):
-                nc.sync.dma_start(
-                    out=w_words[:, j, :].bitcast(I32),
-                    in_=weight_words[g0 + j].rearrange("p n t -> p (n t)").bitcast(I32),
-                )
-            w_words_of.append(w_words)
-
+        w_words = keep.tile([P, GROUPS, COUT], U32, align_bytes=64)
         x_codes = keep.tile([P, GROUPS, COLS], U32, align_bytes=64)
         x_scales = keep.tile([P, GROUPS, COLS], U8, align_bytes=64)
-        for step in range(STEPS):
-            groups = slice(step * STEP, (step + 1) * STEP)
-            grouped = grouped_pool.tile([P, STEP * BATCH, PIXELS, PACK], BF16, align_bytes=64)
-            nc.vector.tensor_copy(
-                out=grouped[:],
-                in_=x_raw_of[step][:].rearrange("p g b (t s) -> p (g b) s t", t=PACK),
-            )
-            nc.vector.quantize_mx(
-                out=x_codes[:, groups, :].rearrange("p g c -> p (g c)").bitcast(FP8X4),
-                scales=x_scales[:, groups, :].rearrange("p g c -> p (g c)"),
-                in_=grouped[:].rearrange("p a s t -> p (a s t)"),
-            )
 
-        acc_of = [psum.tile([P, COLS], F32, name="acc%d" % o) for o in range(O_TILES)]
-        for g in range(GROUPS):
-            step, j = divmod(g, STEP)
-            for o in range(O_TILES):
-                o_cols = slice(o * P, (o + 1) * P)
-                nc.tensor.matmul_mx(
-                    out=acc_of[o][:],
-                    lhsT=w_words_of[step][:, j, o_cols].bitcast(FP8X4),
-                    lhsT_scale=w_scales[ROWS * j : P, step, o_cols],
-                    rhs=x_codes[:, g, :].bitcast(FP8X4),
-                    rhs_scale=x_scales[:, g, :],
-                    start=(g == 0),
-                    stop=(g == GROUPS - 1),
+        with (
+            tc.tile_pool(name="loaded", bufs=3) as loaded_pool,
+            tc.tile_pool(name="flipped", bufs=2) as flipped_pool,
+            tc.tile_pool(name="grouped", bufs=2) as grouped_pool,
+            tc.psum_pool(name="flips", bufs=PER_BANK) as flips,
+        ):
+            batches = [(half, b) for half in range(2) for b in range(BATCH)]
+            loaded_of = []
+            for half, b in batches:
+                loaded = loaded_pool.tile([P, WORDS_C, PACK * PIXELS], BF16)
+                nc.sync.dma_start(
+                    out=loaded[:].rearrange("a c e -> a (c e)"),
+                    in_=x[b, half * HALF * K_PASS : (half + 1) * HALF * K_PASS].rearrange(
+                        "(a r) h w -> a (r h w)", a=P
+                    ),
+                )
+                loaded_of.append(loaded)
+            for g in range(GROUPS):
+                nc.sync.dma_start(
+                    out=w_words[:, g, :].bitcast(I32),
+                    in_=weight_words[g].rearrange("p n t -> p (n t)").bitcast(I32),
                 )
 
-        result = keep.tile([P, O_TILES, COLS], F32)
-        for o in range(O_TILES):
-            if o % 2 == 0:
-                nc.vector.tensor_copy(out=result[:, o, :], in_=acc_of[o][:])
-            else:
-                nc.scalar.copy(out=result[:, o, :], in_=acc_of[o][:])
-        for b in range(BATCH):
-            nc.sync.dma_start(
-                out=out[b].rearrange("(o p) h w -> p o (h w)", p=P),
-                in_=result[:, :, b * PIXELS : (b + 1) * PIXELS],
-            )
+            def leave_psum(turn, out_view, in_view):
+                if turn % 2 == 0:
+                    nc.vector.tensor_copy(out=out_view, in_=in_view)
+                else:
+                    nc.scalar.copy(out=out_view, in_=in_view)
+
+            def first_round(loaded):
+                flipped = flipped_pool.tile([P, P, WORDS_C], F32)
+                for bank_index in range(WORDS_C // PER_BANK):
+                    bank = flips.tile([P, PER_BANK, P], F32, name="first_bank")
+                    for i in range(PER_BANK):
+                        c = bank_index * PER_BANK + i
+                        nc.tensor.transpose(bank[:, i, :], loaded[:, c, :].bitcast(F32), identity[:])
+                    leave_psum(
+                        bank_index // 2,
+                        flipped[:, :, bank_index * PER_BANK : (bank_index + 1) * PER_BANK],
+                        bank[:].rearrange("q c a -> q a c"),
+                    )
+                return flipped
+
+            def second_round(flipped, grouped, b):
+                for bank_index in range(HALF // PER_BANK):
+                    bank = flips.tile([P, PER_BANK, P], F32, name="second_bank")
+                    for i in range(PER_BANK):
+                        g = bank_index * PER_BANK + i
+                        nc.tensor.transpose(
+                            bank[:, i, :],
+                            flipped[:, g * PIECES : (g + 1) * PIECES, :].rearrange("q h c -> q (h c)"),
+                            identity[:],
+                        )
+                    leave_psum(
+                        bank_index,
+                        grouped[:, bank_index * PER_BANK : (bank_index + 1) * PER_BANK, b, :, :],
+                        bank[:].bitcast(BF16).rearrange("p g (t s) -> p g s t", t=PACK),
+                    )
+
+            def quantise(grouped, half):
+                for first in range(0, HALF, QUANT):
+                    groups = slice(half * HALF + first, half * HALF + first + QUANT)
+                    nc.vector.quantize_mx(
+                        out=x_codes[:, groups, :].rearrange("p g c -> p (g c)").bitcast(FP8X4),
+                        scales=x_scales[:, groups, :].rearrange("p g c -> p (g c)"),
+                        in_=grouped[:, first : first + QUANT].rearrange("p g b s t -> p (g b s t)"),
+                    )
+
+            flipped_of = []
+            grouped_of = []
+            for n in range(len(batches) + 1):
+                if n < len(batches):
+                    flipped_of.append(first_round(loaded_of[n]))
+                if n > 0:
+                    half, b = batches[n - 1]
+                    if b == 0:
+                        grouped = grouped_pool.tile([P, HALF, BATCH, PIXELS, PACK], BF16, align_bytes=64)
+                        grouped_of.append(grouped)
+                    second_round(flipped_of[n - 1], grouped_of[half], b)
+                    if b == BATCH - 1:
+                        quantise(grouped_of[half], half)
+
+        with tc.psum_pool(name="sums", bufs=1) as sums, tc.tile_pool(name="last", bufs=1) as last:
+            acc_of = [sums.tile([P, COLS], F32, name="acc%d" % o) for o in range(O_TILES)]
+            for g in range(GROUPS):
+                step, j = divmod(g, STEP)
+                for o in range(O_TILES):
+                    o_cols = slice(o * P, (o + 1) * P)
+                    nc.tensor.matmul_mx(
+                        out=acc_of[o][:],
+                        lhsT=w_words[:, g, o_cols].bitcast(FP8X4),
+                        lhsT_scale=w_scales[ROWS * j : P, step, o_cols],
+                        rhs=x_codes[:, g, :].bitcast(FP8X4),
+                        rhs_scale=x_scales[:, g, :],
+                        start=(g == 0),
+                        stop=(g == GROUPS - 1),
+                    )
+
+            result = last.tile([P, O_TILES, COLS], F32)
+            for o in range(O_TILES):
+                leave_psum(o, result[:, o, :], acc_of[o][:])
+            for b in range(BATCH):
+                nc.sync.dma_start(
+                    out=out[b].rearrange("(o p) h w -> p o (h w)", p=P),
+                    in_=result[:, :, b * PIXELS : (b + 1) * PIXELS],
+                )

@@ -25,6 +25,7 @@ PIECES = P // HALF
 WORDS_C = P // PIECES
 PER_BANK = 4
 QUANT = 4
+LAST_CUTS = 4
 
 FLOPS = 2 * CIN * COUT * COLS
 
@@ -67,10 +68,13 @@ def tile_simpleconvolution_k_kernel(tc, x, weight_words, weight_scales, out):
                 )
                 loaded_of.append(loaded)
             for g in range(GROUPS):
-                nc.sync.dma_start(
-                    out=w_words[:, g, :].bitcast(I32),
-                    in_=weight_words[g].rearrange("p n t -> p (n t)").bitcast(I32),
-                )
+                cuts = LAST_CUTS if g == GROUPS - 1 else 1
+                width = COUT // cuts
+                for first in range(0, COUT, width):
+                    nc.sync.dma_start(
+                        out=w_words[:, g, first : first + width].bitcast(I32),
+                        in_=weight_words[g, :, first : first + width, :].rearrange("p n t -> p (n t)").bitcast(I32),
+                    )
 
             def leave_psum(turn, out_view, in_view):
                 if turn % 2 == 0:
@@ -150,8 +154,7 @@ def tile_simpleconvolution_k_kernel(tc, x, weight_words, weight_scales, out):
             result = last.tile([P, O_TILES, COLS], F32)
             for o in range(O_TILES):
                 leave_psum(o, result[:, o, :], acc_of[o][:])
-            for b in range(BATCH):
                 nc.sync.dma_start(
-                    out=out[b].rearrange("(o p) h w -> p o (h w)", p=P),
-                    in_=result[:, :, b * PIXELS : (b + 1) * PIXELS],
+                    out=out[:, o * P : (o + 1) * P].rearrange("b p h w -> p b (h w)"),
+                    in_=result[:, o, :].rearrange("p (b s) -> p b s", b=BATCH),
                 )

@@ -51,7 +51,7 @@ def tile_simpleconvolution_k_kernel(tc, x, weight_words, weight_scales, out):
         x_scales = keep.tile([P, GROUPS, COLS], U8, align_bytes=64)
 
         with (
-            tc.tile_pool(name="loaded", bufs=3) as loaded_pool,
+            tc.tile_pool(name="loaded", bufs=BATCH * 2) as loaded_pool,
             tc.tile_pool(name="flipped", bufs=2) as flipped_pool,
             tc.tile_pool(name="grouped", bufs=2) as grouped_pool,
             tc.psum_pool(name="flips", bufs=PER_BANK) as flips,

@@ -82,6 +82,8 @@ def tile_simpleconvolution_k_kernel(tc, x, weight_words, weight_scales, out):
                 else:
                     nc.scalar.copy(out=out_view, in_=in_view)
 
+            vector_banks = [(0, 2), (0,)]
+
             def first_round(loaded):
                 flipped = flipped_pool.tile([P, P, WORDS_C], F32)
                 for bank_index in range(WORDS_C // PER_BANK):
@@ -96,7 +98,7 @@ def tile_simpleconvolution_k_kernel(tc, x, weight_words, weight_scales, out):
                     )
                 return flipped
 
-            def second_round(flipped, grouped, b):
+            def second_round(flipped, grouped, half, b):
                 for bank_index in range(HALF // PER_BANK):
                     bank = flips.tile([P, PER_BANK, P], F32, name="second_bank")
                     for i in range(PER_BANK):
@@ -107,19 +109,22 @@ def tile_simpleconvolution_k_kernel(tc, x, weight_words, weight_scales, out):
                             identity[:],
                         )
                     leave_psum(
-                        bank_index,
+                        0 if bank_index in vector_banks[b] else 1,
                         grouped[:, bank_index * PER_BANK : (bank_index + 1) * PER_BANK, b, :, :],
                         bank[:].bitcast(BF16).rearrange("p g (t s) -> p g s t", t=PACK),
                     )
+                    if b == BATCH - 1 and bank_index > 0:
+                        quantise(grouped, half, (bank_index - 1) * QUANT)
+                if b == BATCH - 1:
+                    quantise(grouped, half, HALF - QUANT)
 
-            def quantise(grouped, half):
-                for first in range(0, HALF, QUANT):
-                    groups = slice(half * HALF + first, half * HALF + first + QUANT)
-                    nc.vector.quantize_mx(
-                        out=x_codes[:, groups, :].rearrange("p g c -> p (g c)").bitcast(FP8X4),
-                        scales=x_scales[:, groups, :].rearrange("p g c -> p (g c)"),
-                        in_=grouped[:, first : first + QUANT].rearrange("p g b s t -> p (g b s t)"),
-                    )
+            def quantise(grouped, half, first):
+                groups = slice(half * HALF + first, half * HALF + first + QUANT)
+                nc.vector.quantize_mx(
+                    out=x_codes[:, groups, :].rearrange("p g c -> p (g c)").bitcast(FP8X4),
+                    scales=x_scales[:, groups, :].rearrange("p g c -> p (g c)"),
+                    in_=grouped[:, first : first + QUANT].rearrange("p g b s t -> p (g b s t)"),
+                )
 
             flipped_of = []
             grouped_of = []
@@ -131,9 +136,7 @@ def tile_simpleconvolution_k_kernel(tc, x, weight_words, weight_scales, out):
                     if b == 0:
                         grouped = grouped_pool.tile([P, HALF, BATCH, PIXELS, PACK], BF16, align_bytes=64)
                         grouped_of.append(grouped)
-                    second_round(flipped_of[n - 1], grouped_of[half], b)
-                    if b == BATCH - 1:
-                        quantise(grouped_of[half], half)
+                    second_round(flipped_of[n - 1], grouped_of[half], half, b)
 
         with tc.psum_pool(name="sums", bufs=1) as sums, tc.tile_pool(name="last", bufs=1) as last:
             acc_of = [sums.tile([P, COLS], F32, name="acc%d" % o) for o in range(O_TILES)]

@@ -19,6 +19,7 @@ QUADRANTS = 4
 ROWS = 4
 STEP = 4
 STEPS = GROUPS // STEP
+GPSIMD_STEPS = 6
 
 HALF = GROUPS // 2
 PIECES = P // HALF
@@ -37,14 +38,17 @@ def tile_simpleconvolution_k_kernel(tc, x, weight_words, weight_scales, out):
         nc.vector.memset(w_scales[:].bitcast(I32), 0)
         identity = keep.tile([P, P], F32)
         make_identity(nc, identity[:])
-        for step in range(STEPS):
+        def load_scales(queue, step):
             for quad in range(QUADRANTS):
-                nc.gpsimd.dma_start(
+                queue.dma_start(
                     out=w_scales[32 * quad : 32 * quad + STEP * ROWS, step, :].bitcast(F32),
                     in_=weight_scales[
                         step * STEP : (step + 1) * STEP, ROWS * quad : ROWS * (quad + 1), :
                     ].bitcast(F32),
                 )
+
+        for step in range(GPSIMD_STEPS):
+            load_scales(nc.gpsimd, step)
 
         w_words = keep.tile([P, GROUPS, COUT], U32, align_bytes=64)
         x_codes = keep.tile([P, GROUPS, COLS], U32, align_bytes=64)
@@ -67,6 +71,8 @@ def tile_simpleconvolution_k_kernel(tc, x, weight_words, weight_scales, out):
                     ),
                 )
                 loaded_of.append(loaded)
+            for step in range(GPSIMD_STEPS, STEPS):
+                load_scales(nc.scalar, step)
             for g in range(GROUPS):
                 cuts = LAST_CUTS if g == GROUPS - 1 else 1
                 width = COUT // cuts

from concourse.masks import make_identity
import concourse.mybir as mybir

FP8X4 = mybir.dt.float8_e4m3fn_x4
BF16 = mybir.dt.bfloat16
F32 = mybir.dt.float32
I32 = mybir.dt.int32
U32 = mybir.dt.uint32
U8 = mybir.dt.uint8

P = 128
PACK = 4
K_PASS = P * PACK
BATCH, CIN, COUT, PIXELS = 2, 16384, 1024, 64
GROUPS = CIN // K_PASS
COLS = BATCH * PIXELS
O_TILES = COUT // P
QUADRANTS = 4
ROWS = 4
STEP = 4
STEPS = GROUPS // STEP
GPSIMD_STEPS = 6

HALF = GROUPS // 2
PIECES = P // HALF
WORDS_C = P // PIECES
PER_BANK = 4
QUANT = 4
LAST_CUTS = 4

FLOPS = 2 * CIN * COUT * COLS


def tile_simpleconvolution_k_kernel(tc, x, weight_words, weight_scales, out):
    nc = tc.nc
    with tc.manual_schedule(), tc.tile_pool(name="keep", bufs=1) as keep:
        w_scales = keep.tile([P, STEPS, COUT], U8, align_bytes=64)
        nc.vector.memset(w_scales[:].bitcast(I32), 0)
        identity = keep.tile([P, P], F32)
        make_identity(nc, identity[:])
        def load_scales(queue, step):
            for quad in range(QUADRANTS):
                queue.dma_start(
                    out=w_scales[32 * quad : 32 * quad + STEP * ROWS, step, :].bitcast(F32),
                    in_=weight_scales[
                        step * STEP : (step + 1) * STEP, ROWS * quad : ROWS * (quad + 1), :
                    ].bitcast(F32),
                )

        for step in range(GPSIMD_STEPS):
            load_scales(nc.gpsimd, step)

        w_words = keep.tile([P, GROUPS, COUT], U32, align_bytes=64)
        x_codes = keep.tile([P, GROUPS, COLS], U32, align_bytes=64)
        x_scales = keep.tile([P, GROUPS, COLS], U8, align_bytes=64)

        with (
            tc.tile_pool(name="loaded", bufs=BATCH * 2) as loaded_pool,
            tc.tile_pool(name="flipped", bufs=2) as flipped_pool,
            tc.tile_pool(name="grouped", bufs=2) as grouped_pool,
            tc.psum_pool(name="flips", bufs=PER_BANK) as flips,
        ):
            batches = [(half, b) for half in range(2) for b in range(BATCH)]
            loaded_of = []
            for half, b in batches:
                loaded = loaded_pool.tile([P, WORDS_C, PACK * PIXELS], BF16)
                nc.sync.dma_start(
                    out=loaded[:].rearrange("a c e -> a (c e)"),
                    in_=x[b, half * HALF * K_PASS : (half + 1) * HALF * K_PASS].rearrange(
                        "(a r) h w -> a (r h w)", a=P
                    ),
                )
                loaded_of.append(loaded)
            for step in range(GPSIMD_STEPS, STEPS):
                load_scales(nc.scalar, step)
            for g in range(GROUPS):
                cuts = LAST_CUTS if g == GROUPS - 1 else 1
                width = COUT // cuts
                for first in range(0, COUT, width):
                    nc.sync.dma_start(
                        out=w_words[:, g, first : first + width].bitcast(I32),
                        in_=weight_words[g, :, first : first + width, :].rearrange("p n t -> p (n t)").bitcast(I32),
                    )

            def leave_psum(turn, out_view, in_view):
                if turn % 2 == 0:
                    nc.vector.tensor_copy(out=out_view, in_=in_view)
                else:
                    nc.scalar.copy(out=out_view, in_=in_view)

            vector_banks = [(0, 2), (0,)]

            def first_round(loaded):
                flipped = flipped_pool.tile([P, P, WORDS_C], F32)
                for bank_index in range(WORDS_C // PER_BANK):
                    bank = flips.tile([P, PER_BANK, P], F32, name="first_bank")
                    for i in range(PER_BANK):
                        c = bank_index * PER_BANK + i
                        nc.tensor.transpose(bank[:, i, :], loaded[:, c, :].bitcast(F32), identity[:])
                    leave_psum(
                        bank_index // 2,
                        flipped[:, :, bank_index * PER_BANK : (bank_index + 1) * PER_BANK],
                        bank[:].rearrange("q c a -> q a c"),
                    )
                return flipped

            def second_round(flipped, grouped, half, b):
                for bank_index in range(HALF // PER_BANK):
                    bank = flips.tile([P, PER_BANK, P], F32, name="second_bank")
                    for i in range(PER_BANK):
                        g = bank_index * PER_BANK + i
                        nc.tensor.transpose(
                            bank[:, i, :],
                            flipped[:, g * PIECES : (g + 1) * PIECES, :].rearrange("q h c -> q (h c)"),
                            identity[:],
                        )
                    leave_psum(
                        0 if bank_index in vector_banks[b] else 1,
                        grouped[:, bank_index * PER_BANK : (bank_index + 1) * PER_BANK, b, :, :],
                        bank[:].bitcast(BF16).rearrange("p g (t s) -> p g s t", t=PACK),
                    )
                    if b == BATCH - 1 and bank_index > 0:
                        quantise(grouped, half, (bank_index - 1) * QUANT)
                if b == BATCH - 1:
                    quantise(grouped, half, HALF - QUANT)

            def quantise(grouped, half, first):
                groups = slice(half * HALF + first, half * HALF + first + QUANT)
                nc.vector.quantize_mx(
                    out=x_codes[:, groups, :].rearrange("p g c -> p (g c)").bitcast(FP8X4),
                    scales=x_scales[:, groups, :].rearrange("p g c -> p (g c)"),
                    in_=grouped[:, first : first + QUANT].rearrange("p g b s t -> p (g b s t)"),
                )

            flipped_of = []
            grouped_of = []
            for n in range(len(batches) + 1):
                if n < len(batches):
                    flipped_of.append(first_round(loaded_of[n]))
                if n > 0:
                    half, b = batches[n - 1]
                    if b == 0:
                        grouped = grouped_pool.tile([P, HALF, BATCH, PIXELS, PACK], BF16, align_bytes=64)
                        grouped_of.append(grouped)
                    second_round(flipped_of[n - 1], grouped_of[half], half, b)

        with tc.psum_pool(name="sums", bufs=1) as sums, tc.tile_pool(name="last", bufs=1) as last:
            acc_of = [sums.tile([P, COLS], F32, name="acc%d" % o) for o in range(O_TILES)]
            for g in range(GROUPS):
                step, j = divmod(g, STEP)
                for o in range(O_TILES):
                    o_cols = slice(o * P, (o + 1) * P)
                    nc.tensor.matmul_mx(
                        out=acc_of[o][:],
                        lhsT=w_words[:, g, o_cols].bitcast(FP8X4),
                        lhsT_scale=w_scales[ROWS * j : P, step, o_cols],
                        rhs=x_codes[:, g, :].bitcast(FP8X4),
                        rhs_scale=x_scales[:, g, :],
                        start=(g == 0),
                        stop=(g == GROUPS - 1),
                    )

            result = last.tile([P, O_TILES, COLS], F32)
            for o in range(O_TILES):
                leave_psum(o, result[:, o, :], acc_of[o][:])
                nc.sync.dma_start(
                    out=out[:, o * P : (o + 1) * P].rearrange("b p h w -> p b (h w)"),
                    in_=result[:, o, :].rearrange("p (b s) -> p b s", b=BATCH),
                )
